import numpy as np
import ml_dtypes


def mxq(x, axis, fmt="e4m3"):
    dtype, down = {"e4m3": (ml_dtypes.float8_e4m3fn, 7), "e5m2": (ml_dtypes.float8_e5m2, 14)}[fmt]
    v = np.moveaxis(np.asarray(x, np.float32).astype(ml_dtypes.bfloat16).astype(np.float64), axis, -1)
    blocks = v.reshape(v.shape[:-1] + (-1, 32))
    amax = np.abs(blocks).max(-1, keepdims=True)
    byte = np.maximum(np.where(amax > 0, np.frexp(amax)[1] - 1 + 127, 0) - down, 1)
    scale = np.exp2(byte - 127.0)
    codes = (blocks / scale).astype(np.float32).astype(dtype).astype(np.float64)
    return np.moveaxis((codes * scale).reshape(v.shape), -1, axis)


WIDE = False


def mx_kscale(k):
    if not WIDE:
        return np.ones(k)
    levels = np.array([10, -10, 5, -5, 0])
    a = np.random.permutation(np.resize(levels, k // 512 * 4)).reshape(k // 512, 4)
    idx = np.arange(k)
    return np.exp2(a[idx // 512, idx % 128 // 32])


BF16 = ml_dtypes.bfloat16


def bf(x):
    return np.asarray(x, np.float32).astype(BF16)


def f64(x):
    return np.asarray(x).astype(np.float64)


N, C, HH, WW = 4, 512, 32, 32
S = HH * WW
EPS = 1e-5


def setup_inputs():
    s = mx_kscale(C)
    contrast = np.exp2(np.random.uniform(-8.0, 1.0, (N, 1, HH, WW)))
    shift = 0.5 * np.random.standard_normal((N, 1, HH, WW))
    w = 1.0 / np.sqrt(C)
    return {"x": bf(contrast * (np.random.standard_normal((N, C, HH, WW)) + shift)),
            "ln_gamma": bf((1.0 + 0.1 * np.random.standard_normal(C)) * s),
            "ln_beta": bf(0.3 * np.random.standard_normal(C) * s),
            "Wq": bf(np.random.standard_normal((C, C)) * w / s[None, :]),
            "bq": bf(0.3 * np.random.standard_normal(C)),
            "Wk": bf(np.random.standard_normal((C, C)) * w / s[None, :]),
            "bk": bf(0.3 * np.random.standard_normal(C)),
            "Wv": bf(np.random.standard_normal((C, C)) * w / s[None, :]),
            "bv": bf(0.3 * np.random.standard_normal(C))}


def reference(x, ln_gamma, ln_beta, Wq, bq, Wk, bk, Wv, bv):
    xs = f64(x).reshape(N, C, S).swapaxes(1, 2)
    mu = xs.mean(-1, keepdims=True)
    var = xs.var(-1, keepdims=True)
    x_ln = (xs - mu) / np.sqrt(var + EPS) * f64(ln_gamma) + f64(ln_beta)
    xq = mxq(x_ln, 2, "e4m3")
    q = (xq @ mxq(f64(Wq), 1, "e4m3").T) + f64(bq)
    k = (xq @ mxq(f64(Wk), 1, "e4m3").T) + f64(bk)
    v = (xq @ mxq(f64(Wv), 1, "e4m3").T) + f64(bv)
    return q, k, v

@@ -1,0 +1,267 @@
+from contextlib import ExitStack
+
+import concourse.mybir as mybir
+from concourse.masks import make_identity
+
+F32 = mybir.dt.float32
+BF16 = mybir.dt.bfloat16
+U32 = mybir.dt.uint32
+U8 = mybir.dt.uint8
+FP8X4 = mybir.dt.float8_e4m3fn_x4
+ACT = mybir.ActivationFunctionType
+ALU = mybir.AluOpType
+
+P = 128
+PACK = 4
+IMAGES = 4
+C = 512
+PIXELS = 1024
+GROUP = 512
+TILES = GROUP // P
+GROUPS = IMAGES * PIXELS // GROUP
+UNITS = 3 * GROUPS
+EPS = 1e-5
+
+FLOPS = 2 * IMAGES * PIXELS * C * 3 * C
+
+
+def tile_selfscaleddotproductattention2d_pa_t_kernel(
+    tc, x, ln_gamma, ln_beta, Wq, bq, Wk, bk, Wv, bv, out_0, out_1, out_2
+):
+    nc = tc.nc
+    weights = [Wq, Wk, Wv]
+    biases = [bq, bk, bv]
+    outs = [out_0, out_1, out_2]
+
+    with ExitStack() as ctx:
+        ctx.enter_context(tc.manual_schedule())
+        keep = ctx.enter_context(tc.tile_pool(name="keep", bufs=1))
+        small = ctx.enter_context(tc.tile_pool(name="small", bufs=3))
+        work = ctx.enter_context(tc.tile_pool(name="work", bufs=2))
+        results = ctx.enter_context(tc.tile_pool(name="results", bufs=6))
+        psum_pixel = ctx.enter_context(tc.psum_pool(name="psum_pixel", bufs=2))
+        psum_plane = ctx.enter_context(tc.psum_pool(name="psum_plane", bufs=2))
+        psum_out = ctx.enter_context(tc.psum_pool(name="psum_out", bufs=4))
+
+        x_sb = []
+        w_sb = []
+        for n in range(IMAGES):
+            x_sb.append(keep.tile([P, PACK, PIXELS], BF16, name="x_sb%d" % n))
+        for w in range(3):
+            w_sb.append(keep.tile([P, C // P, C], BF16, name="w_sb%d" % w))
+        nc.sync.dma_start(out=x_sb[0][:], in_=x[0].rearrange("(p j) h w -> p j (h w)", j=PACK))
+        for w in range(3):
+            nc.sync.dma_start(out=w_sb[w][:], in_=weights[w].rearrange("(a p) c -> p a c", p=P))
+        for n in range(1, IMAGES):
+            nc.sync.dma_start(out=x_sb[n][:], in_=x[n].rearrange("(p j) h w -> p j (h w)", j=PACK))
+
+        gamma_bf = keep.tile([P, PACK], BF16, name="gamma_bf")
+        beta_bf = keep.tile([P, PACK], BF16, name="beta_bf")
+        bias_bc = keep.tile([P, 3, C], BF16, name="bias_bc")
+        with nc.allow_non_contiguous_dma(reason="four channels of gain and shift to a partition"):
+            nc.scalar.dma_start(out=gamma_bf[:], in_=ln_gamma.rearrange("(p j) -> p j", j=PACK))
+            nc.scalar.dma_start(out=beta_bf[:], in_=ln_beta.rearrange("(p j) -> p j", j=PACK))
+        for w in range(3):
+            nc.scalar.dma_start(out=bias_bc[:, w, :], in_=biases[w].partition_broadcast(P))
+
+        ident_bf = keep.tile([P, P], BF16, name="ident_bf")
+        ident_f32 = keep.tile([P, P], F32, name="ident_f32")
+        make_identity(nc, ident_bf[:])
+        make_identity(nc, ident_f32[:])
+        gamma = keep.tile([P, PACK], F32, name="gamma")
+        beta = keep.tile([P, PACK], F32, name="beta")
+        nc.vector.tensor_copy(out=gamma[:], in_=gamma_bf[:])
+        nc.vector.tensor_copy(out=beta[:], in_=beta_bf[:])
+
+        w_codes = keep.tile([P, 3, C], U32, name="w_codes", align_bytes=64)
+        w_scales = keep.tile([P, 3, C], U8, name="w_scales", align_bytes=64)
+
+        def prepare_weight(w):
+            words = w_sb[w][:].bitcast(F32).rearrange("p a (q u) -> p a u q", u=2)
+            w_grouped = keep.tile([P, C, PACK], BF16, name="w_grouped%d" % w, align_bytes=64)
+            pairs = w_grouped[:].bitcast(F32)
+            for half in range(2):
+                bank = psum_plane.tile([P, 2, 2 * P], F32, name="w_bank", tag="plane")
+                for a in range(2):
+                    for u in range(2):
+                        nc.tensor.transpose(
+                            bank[:, u, a * P : (a + 1) * P], words[:, 2 * half + a, u, :], ident_f32[:]
+                        )
+                nc.vector.tensor_copy(
+                    out=pairs[:, 2 * half * P : 2 * (half + 1) * P, :],
+                    in_=bank[:].rearrange("p u o -> p o u"),
+                )
+            nc.vector.quantize_mx(
+                out=w_codes[:, w, :].bitcast(FP8X4),
+                scales=w_scales[:, w, :],
+                in_=w_grouped[:].rearrange("p o t -> p (o t)"),
+            )
+
+        x_t = {}
+        mean_var = {}
+        rstd = {}
+        shift = {}
+        x_hat = {}
+        plane_bank = {}
+        planes = {}
+        codes = {}
+        scales = {}
+        acc = {}
+        result = {}
+
+        def to_pixel_layout(g):
+            n, half = divmod(g, PIXELS // GROUP)
+            x_t[g] = []
+            for b in range(TILES // 2):
+                x_t[g].append(psum_pixel.tile([P, 2, PACK, P], BF16, name="x_t", tag="x_t"))
+            for i in range(TILES):
+                first = half * GROUP + i * P
+                for j in range(PACK):
+                    nc.tensor.transpose(
+                        x_t[g][i // 2][:, i % 2, j, :], x_sb[n][:, j, first : first + P], ident_bf[:]
+                    )
+
+        def statistics(g, bank):
+            if bank == 0:
+                mean_var[g] = small.tile([P, TILES, 2], F32, name="mean_var")
+            for i in (2 * bank, 2 * bank + 1):
+                stats = small.tile([P, 6], F32, name="stats")
+                nc.vector.bn_stats(out=stats[:], in_=x_t[g][bank][:, i % 2].rearrange("p j c -> p (j c)"))
+                nc.vector.bn_aggr(out=mean_var[g][:, i, :], in_=stats[:])
+
+        def scale_and_shift(g):
+            var_eps = small.tile([P, TILES], F32, name="var_eps")
+            std = small.tile([P, TILES], F32, name="std")
+            rstd[g] = small.tile([P, TILES], F32, name="rstd")
+            shift[g] = small.tile([P, TILES], F32, name="shift")
+            nc.vector.tensor_scalar_add(out=var_eps[:], in0=mean_var[g][:, :, 1], scalar1=EPS)
+            nc.scalar.sqrt(out=std[:], in_=var_eps[:])
+            nc.vector.reciprocal(out=rstd[g][:], in_=std[:])
+            nc.vector.scalar_tensor_tensor(
+                out=shift[g][:], in0=mean_var[g][:, :, 0], scalar=-1.0, in1=rstd[g][:],
+                op0=ALU.mult, op1=ALU.mult,
+            )
+
+        def normalise(g):
+            x_hat[g] = work.tile([P, TILES, PACK, P], F32, name="x_hat")
+            for i in range(TILES):
+                nc.scalar.activation(
+                    out=x_hat[g][:, i],
+                    in_=x_t[g][i // 2][:, i % 2],
+                    func=ACT.Identity,
+                    scale=rstd[g][:, i : i + 1],
+                    bias=shift[g][:, i : i + 1],
+                )
+
+        def to_channel_layout(g, j):
+            plane_bank[g, j] = psum_plane.tile([P, GROUP], F32, name="plane", tag="plane")
+            for i in range(TILES):
+                nc.tensor.transpose(
+                    plane_bank[g, j][:, i * P : (i + 1) * P], x_hat[g][:, i, j, :], ident_f32[:]
+                )
+
+        def gain_and_shift(g, j):
+            if j == 0:
+                planes[g] = work.tile([P, PACK, GROUP], BF16, name="planes")
+            nc.scalar.activation(
+                out=planes[g][:, j, :].rearrange("p (s q) -> p s q", s=TILES),
+                in_=plane_bank[g, j][:].rearrange("p (q s) -> p s q", s=TILES),
+                func=ACT.Identity,
+                scale=gamma[:, j : j + 1],
+                bias=beta[:, j : j + 1],
+            )
+
+        def regroup_and_quantise(g):
+            grouped = work.tile([P, GROUP, PACK], BF16, name="grouped", align_bytes=64)
+            nc.vector.tensor_copy(
+                out=grouped[:].rearrange("p (c i) j -> p c j i", i=4),
+                in_=planes[g][:].rearrange("p j (c i) -> p c j i", i=4),
+            )
+            codes[g] = work.tile([P, GROUP], U32, name="codes", align_bytes=64)
+            scales[g] = work.tile([P, GROUP], U8, name="scales", align_bytes=64)
+            nc.vector.quantize_mx(
+                out=codes[g][:].bitcast(FP8X4),
+                scales=scales[g][:],
+                in_=grouped[:].rearrange("p w j -> p (w j)"),
+            )
+
+        def multiply(u, s):
+            g, w = divmod(u, 3)
+            acc[u, s] = psum_out.tile([P, C], F32, name="acc")
+            nc.tensor.matmul_mx(
+                out=acc[u, s][:],
+                lhsT=codes[g][:, s * P : (s + 1) * P].bitcast(FP8X4),
+                lhsT_scale=scales[g][:, s * P : (s + 1) * P],
+                rhs=w_codes[:, w, :].bitcast(FP8X4),
+                rhs_scale=w_scales[:, w, :],
+                start=True,
+                stop=True,
+            )
+
+        def evacuate(u, s):
+            w = u % 3
+            if s == 0:
+                result[u] = results.tile([P, TILES, C], F32, name="result")
+            if s % 2 == 0:
+                nc.vector.tensor_tensor(
+                    out=result[u][:, s, :], in0=acc[u, s][:], in1=bias_bc[:, w, :], op=ALU.add
+                )
+            else:
+                nc.scalar.copy(out=result[u][:, s, :], in_=acc[u, s][:])
+                nc.gpsimd.tensor_tensor(
+                    out=result[u][:, s, :], in0=result[u][:, s, :], in1=bias_bc[:, w, :], op=ALU.add
+                )
+
+        def store(u):
+            g, w = divmod(u, 3)
+            n, half = divmod(g, PIXELS // GROUP)
+            rows = slice(half * GROUP, (half + 1) * GROUP)
+            nc.sync.dma_start(
+                out=outs[w][n, rows, :].rearrange("(q s) o -> q s o", s=TILES), in_=result[u][:]
+            )
+
+        def finish_unit(u):
+            for s in range(TILES):
+                if 0 <= u < UNITS:
+                    evacuate(u, s)
+                if 0 <= u + 1 < UNITS:
+                    multiply(u + 1, s)
+            if 0 <= u < UNITS:
+                store(u)
+
+        def is_group(g):
+            return 0 <= g < GROUPS
+
+        to_pixel_layout(0)
+        statistics(0, 0)
+        statistics(0, 1)
+        scale_and_shift(0)
+        for w in range(3):
+            prepare_weight(w)
+
+        for r in range(GROUPS + 2):
+            if is_group(r):
+                normalise(r)
+            if is_group(r - 1):
+                regroup_and_quantise(r - 1)
+            if is_group(r + 1):
+                to_pixel_layout(r + 1)
+            if is_group(r):
+                to_channel_layout(r, 0)
+                to_channel_layout(r, 1)
+            finish_unit(3 * (r - 2) + 2)
+            if is_group(r):
+                gain_and_shift(r, 0)
+                gain_and_shift(r, 1)
+                to_channel_layout(r, 2)
+                to_channel_layout(r, 3)
+            if is_group(r + 1):
+                statistics(r + 1, 0)
+            finish_unit(3 * (r - 1))
+            if is_group(r):
+                gain_and_shift(r, 2)
+                gain_and_shift(r, 3)
+            if is_group(r + 1):
+                statistics(r + 1, 1)
+                scale_and_shift(r + 1)
+            finish_unit(3 * (r - 1) + 1)

@@ -16,7 +16,7 @@ PACK = 4
 IMAGES = 4
 C = 512
 PIXELS = 1024
-GROUP = 512
+GROUP = 256
 TILES = GROUP // P
 GROUPS = IMAGES * PIXELS // GROUP
 UNITS = 3 * GROUPS
@@ -41,7 +41,7 @@ def tile_selfscaleddotproductattention2d_pa_t_kernel(
         results = ctx.enter_context(tc.tile_pool(name="results", bufs=6))
         psum_pixel = ctx.enter_context(tc.psum_pool(name="psum_pixel", bufs=2))
         psum_plane = ctx.enter_context(tc.psum_pool(name="psum_plane", bufs=2))
-        psum_out = ctx.enter_context(tc.psum_pool(name="psum_out", bufs=4))
+        psum_out = ctx.enter_context(tc.psum_pool(name="psum_out", bufs=2 * TILES))
 
         x_sb = []
         w_sb = []
@@ -81,13 +81,13 @@ def tile_selfscaleddotproductattention2d_pa_t_kernel(
             w_grouped = keep.tile([P, C, PACK], BF16, name="w_grouped%d" % w, align_bytes=64)
             pairs = w_grouped[:].bitcast(F32)
             for half in range(2):
-                bank = psum_plane.tile([P, 2, 2 * P], F32, name="w_bank", tag="plane")
+                bank = psum_out.tile([P, 2, 2 * P], F32, name="w_bank", tag="acc")
                 for a in range(2):
                     for u in range(2):
                         nc.tensor.transpose(
                             bank[:, u, a * P : (a + 1) * P], words[:, 2 * half + a, u, :], ident_f32[:]
                         )
-                nc.vector.tensor_copy(
+                nc.scalar.copy(
                     out=pairs[:, 2 * half * P : 2 * (half + 1) * P, :],
                     in_=bank[:].rearrange("p u o -> p o u"),
                 )
@@ -99,6 +99,8 @@ def tile_selfscaleddotproductattention2d_pa_t_kernel(
 
         x_t = {}
         mean_var = {}
+        var_eps = {}
+        std = {}
         rstd = {}
         shift = {}
         x_hat = {}
@@ -107,36 +109,32 @@ def tile_selfscaleddotproductattention2d_pa_t_kernel(
         codes = {}
         scales = {}
         acc = {}
-        result = {}
 
         def to_pixel_layout(g):
-            n, half = divmod(g, PIXELS // GROUP)
-            x_t[g] = []
-            for b in range(TILES // 2):
-                x_t[g].append(psum_pixel.tile([P, 2, PACK, P], BF16, name="x_t", tag="x_t"))
+            n, part = divmod(g, PIXELS // GROUP)
+            x_t[g] = psum_pixel.tile([P, TILES, PACK, P], BF16, name="x_t")
             for i in range(TILES):
-                first = half * GROUP + i * P
+                first = part * GROUP + i * P
                 for j in range(PACK):
-                    nc.tensor.transpose(
-                        x_t[g][i // 2][:, i % 2, j, :], x_sb[n][:, j, first : first + P], ident_bf[:]
-                    )
+                    nc.tensor.transpose(x_t[g][:, i, j, :], x_sb[n][:, j, first : first + P], ident_bf[:])
 
-        def statistics(g, bank):
-            if bank == 0:
-                mean_var[g] = small.tile([P, TILES, 2], F32, name="mean_var")
-            for i in (2 * bank, 2 * bank + 1):
+        def statistics(g):
+            mean_var[g] = small.tile([P, TILES, 2], F32, name="mean_var")
+            var_eps[g] = small.tile([P, TILES], F32, name="var_eps")
+            for i in range(TILES):
                 stats = small.tile([P, 6], F32, name="stats")
-                nc.vector.bn_stats(out=stats[:], in_=x_t[g][bank][:, i % 2].rearrange("p j c -> p (j c)"))
+                nc.vector.bn_stats(out=stats[:], in_=x_t[g][:, i].rearrange("p j c -> p (j c)"))
                 nc.vector.bn_aggr(out=mean_var[g][:, i, :], in_=stats[:])
+            nc.vector.tensor_scalar_add(out=var_eps[g][:], in0=mean_var[g][:, :, 1], scalar1=EPS)
+
+        def root(g):
+            std[g] = small.tile([P, TILES], F32, name="std")
+            nc.scalar.sqrt(out=std[g][:], in_=var_eps[g][:])
 
         def scale_and_shift(g):
-            var_eps = small.tile([P, TILES], F32, name="var_eps")
-            std = small.tile([P, TILES], F32, name="std")
             rstd[g] = small.tile([P, TILES], F32, name="rstd")
             shift[g] = small.tile([P, TILES], F32, name="shift")
-            nc.vector.tensor_scalar_add(out=var_eps[:], in0=mean_var[g][:, :, 1], scalar1=EPS)
-            nc.scalar.sqrt(out=std[:], in_=var_eps[:])
-            nc.vector.reciprocal(out=rstd[g][:], in_=std[:])
+            nc.vector.reciprocal(out=rstd[g][:], in_=std[g][:])
             nc.vector.scalar_tensor_tensor(
                 out=shift[g][:], in0=mean_var[g][:, :, 0], scalar=-1.0, in1=rstd[g][:],
                 op0=ALU.mult, op1=ALU.mult,
@@ -147,29 +145,32 @@ def tile_selfscaleddotproductattention2d_pa_t_kernel(
             for i in range(TILES):
                 nc.scalar.activation(
                     out=x_hat[g][:, i],
-                    in_=x_t[g][i // 2][:, i % 2],
+                    in_=x_t[g][:, i],
                     func=ACT.Identity,
                     scale=rstd[g][:, i : i + 1],
                     bias=shift[g][:, i : i + 1],
                 )
 
-        def to_channel_layout(g, j):
-            plane_bank[g, j] = psum_plane.tile([P, GROUP], F32, name="plane", tag="plane")
-            for i in range(TILES):
-                nc.tensor.transpose(
-                    plane_bank[g, j][:, i * P : (i + 1) * P], x_hat[g][:, i, j, :], ident_f32[:]
-                )
+        def to_channel_layout(g):
+            for b in range(2):
+                plane_bank[g, b] = psum_plane.tile([P, 2, GROUP], F32, name="plane")
+                for j in (2 * b, 2 * b + 1):
+                    for i in range(TILES):
+                        nc.tensor.transpose(
+                            plane_bank[g, b][:, j % 2, i * P : (i + 1) * P], x_hat[g][:, i, j, :], ident_f32[:]
+                        )
 
-        def gain_and_shift(g, j):
-            if j == 0:
+        def gain_and_shift(g, b):
+            if b == 0:
                 planes[g] = work.tile([P, PACK, GROUP], BF16, name="planes")
-            nc.scalar.activation(
-                out=planes[g][:, j, :].rearrange("p (s q) -> p s q", s=TILES),
-                in_=plane_bank[g, j][:].rearrange("p (q s) -> p s q", s=TILES),
-                func=ACT.Identity,
-                scale=gamma[:, j : j + 1],
-                bias=beta[:, j : j + 1],
-            )
+            for j in (2 * b, 2 * b + 1):
+                nc.scalar.activation(
+                    out=planes[g][:, j, :].rearrange("p (s q) -> p s q", s=TILES),
+                    in_=plane_bank[g, b][:, j % 2, :].rearrange("p (q s) -> p s q", s=TILES),
+                    func=ACT.Identity,
+                    scale=gamma[:, j : j + 1],
+                    bias=beta[:, j : j + 1],
+                )
 
         def regroup_and_quantise(g):
             grouped = work.tile([P, GROUP, PACK], BF16, name="grouped", align_bytes=64)
@@ -185,83 +186,63 @@ def tile_selfscaleddotproductattention2d_pa_t_kernel(
                 in_=grouped[:].rearrange("p w j -> p (w j)"),
             )
 
-        def multiply(u, s):
+        def start_unit(u):
             g, w = divmod(u, 3)
-            acc[u, s] = psum_out.tile([P, C], F32, name="acc")
-            nc.tensor.matmul_mx(
-                out=acc[u, s][:],
-                lhsT=codes[g][:, s * P : (s + 1) * P].bitcast(FP8X4),
-                lhsT_scale=scales[g][:, s * P : (s + 1) * P],
-                rhs=w_codes[:, w, :].bitcast(FP8X4),
-                rhs_scale=w_scales[:, w, :],
-                start=True,
-                stop=True,
-            )
-
-        def evacuate(u, s):
-            w = u % 3
-            if s == 0:
-                result[u] = results.tile([P, TILES, C], F32, name="result")
-            if s % 2 == 0:
-                nc.vector.tensor_tensor(
-                    out=result[u][:, s, :], in0=acc[u, s][:], in1=bias_bc[:, w, :], op=ALU.add
+            for s in range(TILES):
+                acc[u, s] = psum_out.tile([P, C], F32, name="acc")
+                nc.tensor.matmul_mx(
+                    out=acc[u, s][:],
+                    lhsT=codes[g][:, s * P : (s + 1) * P].bitcast(FP8X4),
+                    lhsT_scale=scales[g][:, s * P : (s + 1) * P],
+                    rhs=w_codes[:, w, :].bitcast(FP8X4),
+                    rhs_scale=w_scales[:, w, :],
+                    start=True,
+                    stop=True,
                 )
-            else:
-                nc.scalar.copy(out=result[u][:, s, :], in_=acc[u, s][:])
-                nc.gpsimd.tensor_tensor(
-                    out=result[u][:, s, :], in0=result[u][:, s, :], in1=bias_bc[:, w, :], op=ALU.add
-                )
-
-        def store(u):
-            g, w = divmod(u, 3)
-            n, half = divmod(g, PIXELS // GROUP)
-            rows = slice(half * GROUP, (half + 1) * GROUP)
-            nc.sync.dma_start(
-                out=outs[w][n, rows, :].rearrange("(q s) o -> q s o", s=TILES), in_=result[u][:]
-            )
 
         def finish_unit(u):
-            for s in range(TILES):
-                if 0 <= u < UNITS:
-                    evacuate(u, s)
-                if 0 <= u + 1 < UNITS:
-                    multiply(u + 1, s)
+            g, w = divmod(u, 3)
+            n, part = divmod(g, PIXELS // GROUP)
+            rows = slice(part * GROUP, (part + 1) * GROUP)
+            result = results.tile([P, TILES, C], F32, name="result")
+            nc.vector.tensor_tensor(out=result[:, 0, :], in0=acc[u, 0][:], in1=bias_bc[:, w, :], op=ALU.add)
+            nc.scalar.copy(out=result[:, 1, :], in_=acc[u, 1][:])
+            nc.gpsimd.tensor_tensor(out=result[:, 1, :], in0=result[:, 1, :], in1=bias_bc[:, w, :], op=ALU.add)
+            nc.sync.dma_start(out=outs[w][n, rows, :].rearrange("(q s) o -> q s o", s=TILES), in_=result[:])
+
+        def turn_over(u):
+            if 0 <= u - 2 < UNITS:
+                finish_unit(u - 2)
             if 0 <= u < UNITS:
-                store(u)
+                start_unit(u)
 
         def is_group(g):
             return 0 <= g < GROUPS
 
-        to_pixel_layout(0)
-        statistics(0, 0)
-        statistics(0, 1)
-        scale_and_shift(0)
-        for w in range(3):
-            prepare_weight(w)
-
-        for r in range(GROUPS + 2):
+        for r in range(-2, GROUPS + 3):
             if is_group(r):
                 normalise(r)
+            if is_group(r - 2):
+                regroup_and_quantise(r - 2)
+            if is_group(r + 2):
+                to_pixel_layout(r + 2)
+            turn_over(3 * (r - 2))
+
+            if is_group(r + 1):
+                root(r + 1)
             if is_group(r - 1):
-                regroup_and_quantise(r - 1)
+                gain_and_shift(r - 1, 0)
             if is_group(r + 1):
-                to_pixel_layout(r + 1)
-            if is_group(r):
-                to_channel_layout(r, 0)
-                to_channel_layout(r, 1)
-            finish_unit(3 * (r - 2) + 2)
-            if is_group(r):
-                gain_and_shift(r, 0)
-                gain_and_shift(r, 1)
-                to_channel_layout(r, 2)
-                to_channel_layout(r, 3)
-            if is_group(r + 1):
-                statistics(r + 1, 0)
-            finish_unit(3 * (r - 1))
-            if is_group(r):
-                gain_and_shift(r, 2)
-                gain_and_shift(r, 3)
-            if is_group(r + 1):
-                statistics(r + 1, 1)
                 scale_and_shift(r + 1)
-            finish_unit(3 * (r - 1) + 1)
+            turn_over(3 * (r - 2) + 1)
+
+            if is_group(r - 1):
+                gain_and_shift(r - 1, 1)
+            if is_group(r + 2):
+                statistics(r + 2)
+            if is_group(r):
+                to_channel_layout(r)
+            turn_over(3 * (r - 2) + 2)
+
+            if 0 <= r + 1 < 3:
+                prepare_weight(r + 1)

@@ -41,7 +41,8 @@ def tile_selfscaleddotproductattention2d_pa_t_kernel(
         results = ctx.enter_context(tc.tile_pool(name="results", bufs=6))
         psum_pixel = ctx.enter_context(tc.psum_pool(name="psum_pixel", bufs=2))
         psum_plane = ctx.enter_context(tc.psum_pool(name="psum_plane", bufs=2))
-        psum_out = ctx.enter_context(tc.psum_pool(name="psum_out", bufs=2 * TILES))
+        psum_sums = ctx.enter_context(tc.psum_pool(name="psum_sums", bufs=1))
+        psum_out = ctx.enter_context(tc.psum_pool(name="psum_out", bufs=3))
 
         x_sb = []
         w_sb = []
@@ -68,6 +69,14 @@ def tile_selfscaleddotproductattention2d_pa_t_kernel(
         ident_f32 = keep.tile([P, P], F32, name="ident_f32")
         make_identity(nc, ident_bf[:])
         make_identity(nc, ident_f32[:])
+        ones_bf = keep.tile([P, 2], BF16, name="ones_bf")
+        one = keep.tile([P, 1], F32, name="one")
+        eps = keep.tile([P, 1], F32, name="eps")
+        warm = keep.tile([P, 1], F32, name="warm")
+        nc.vector.memset(ones_bf[:], 1.0)
+        nc.vector.memset(one[:], 1.0)
+        nc.vector.tensor_scalar_mul(out=eps[:], in0=one[:], scalar1=EPS)
+        nc.scalar.sqrt(out=warm[:], in_=one[:])
         gamma = keep.tile([P, PACK], F32, name="gamma")
         beta = keep.tile([P, PACK], F32, name="beta")
         nc.vector.tensor_copy(out=gamma[:], in_=gamma_bf[:])
@@ -98,47 +107,64 @@ def tile_selfscaleddotproductattention2d_pa_t_kernel(
             )
 
         x_t = {}
-        mean_var = {}
-        var_eps = {}
+        sums = {}
+        minus_mean = {}
+        squares = {}
         std = {}
         rstd = {}
         shift = {}
         x_hat = {}
         plane_bank = {}
         planes = {}
+        grouped = {}
         codes = {}
         scales = {}
         acc = {}
+        result = {}
 
         def to_pixel_layout(g):
             n, part = divmod(g, PIXELS // GROUP)
             x_t[g] = psum_pixel.tile([P, TILES, PACK, P], BF16, name="x_t")
+            sums[g] = psum_sums.tile([P, TILES, 2], F32, name="sums")
             for i in range(TILES):
                 first = part * GROUP + i * P
                 for j in range(PACK):
                     nc.tensor.transpose(x_t[g][:, i, j, :], x_sb[n][:, j, first : first + P], ident_bf[:])
-
-        def statistics(g):
-            mean_var[g] = small.tile([P, TILES, 2], F32, name="mean_var")
-            var_eps[g] = small.tile([P, TILES], F32, name="var_eps")
             for i in range(TILES):
-                stats = small.tile([P, 6], F32, name="stats")
-                nc.vector.bn_stats(out=stats[:], in_=x_t[g][:, i].rearrange("p j c -> p (j c)"))
-                nc.vector.bn_aggr(out=mean_var[g][:, i, :], in_=stats[:])
-            nc.vector.tensor_scalar_add(out=var_eps[g][:], in0=mean_var[g][:, :, 1], scalar1=EPS)
+                first = part * GROUP + i * P
+                for j in range(PACK):
+                    nc.tensor.matmul(
+                        out=sums[g][:, i, :],
+                        lhsT=x_sb[n][:, j, first : first + P],
+                        rhs=ones_bf[:],
+                        start=(j == 0),
+                        stop=(j == PACK - 1),
+                    )
 
-        def root(g):
+        def centre(g):
+            minus_mean[g] = small.tile([P, TILES], F32, name="minus_mean")
+            nc.vector.tensor_scalar_mul(out=minus_mean[g][:], in0=sums[g][:, :, 0], scalar1=-1.0 / C)
+
+        def deviation(g):
+            squares[g] = small.tile([P, TILES], F32, name="squares")
             std[g] = small.tile([P, TILES], F32, name="std")
-            nc.scalar.sqrt(out=std[g][:], in_=var_eps[g][:])
+            for i in range(TILES):
+                unused = work.tile([P, PACK, P], BF16, name="unused")
+                nc.scalar.activation(
+                    out=unused[:],
+                    in_=x_t[g][:, i],
+                    func=ACT.Square,
+                    bias=minus_mean[g][:, i : i + 1],
+                    scale=1.0,
+                    accum_out=squares[g][:, i : i + 1],
+                )
+            nc.scalar.activation(out=std[g][:], in_=squares[g][:], func=ACT.Sqrt, bias=eps[:], scale=1.0 / C)
 
         def scale_and_shift(g):
             rstd[g] = small.tile([P, TILES], F32, name="rstd")
             shift[g] = small.tile([P, TILES], F32, name="shift")
             nc.vector.reciprocal(out=rstd[g][:], in_=std[g][:])
-            nc.vector.scalar_tensor_tensor(
-                out=shift[g][:], in0=mean_var[g][:, :, 0], scalar=-1.0, in1=rstd[g][:],
-                op0=ALU.mult, op1=ALU.mult,
-            )
+            nc.vector.tensor_tensor(out=shift[g][:], in0=minus_mean[g][:], in1=rstd[g][:], op=ALU.mult)
 
         def normalise(g):
             x_hat[g] = work.tile([P, TILES, PACK, P], F32, name="x_hat")
@@ -160,61 +186,66 @@ def tile_selfscaleddotproductattention2d_pa_t_kernel(
                             plane_bank[g, b][:, j % 2, i * P : (i + 1) * P], x_hat[g][:, i, j, :], ident_f32[:]
                         )
 
-        def gain_and_shift(g, b):
-            if b == 0:
-                planes[g] = work.tile([P, PACK, GROUP], BF16, name="planes")
-            for j in (2 * b, 2 * b + 1):
+        def gain_and_shift(g):
+            planes[g] = work.tile([P, PACK, GROUP], BF16, name="planes")
+            for j in range(PACK):
                 nc.scalar.activation(
                     out=planes[g][:, j, :].rearrange("p (s q) -> p s q", s=TILES),
-                    in_=plane_bank[g, b][:, j % 2, :].rearrange("p (q s) -> p s q", s=TILES),
+                    in_=plane_bank[g, j // 2][:, j % 2, :].rearrange("p (q s) -> p s q", s=TILES),
                     func=ACT.Identity,
                     scale=gamma[:, j : j + 1],
                     bias=beta[:, j : j + 1],
                 )
 
-        def regroup_and_quantise(g):
-            grouped = work.tile([P, GROUP, PACK], BF16, name="grouped", align_bytes=64)
-            nc.vector.tensor_copy(
-                out=grouped[:].rearrange("p (c i) j -> p c j i", i=4),
-                in_=planes[g][:].rearrange("p j (c i) -> p c j i", i=4),
+        def regroup(g, s, copy):
+            if s == TILES - 1:
+                grouped[g] = work.tile([P, GROUP, PACK], BF16, name="grouped", align_bytes=64)
+            cols = slice(s * P, (s + 1) * P)
+            copy(
+                out=grouped[g][:, cols, :].rearrange("p (c i) j -> p c j i", i=4),
+                in_=planes[g][:, :, cols].rearrange("p j (c i) -> p c j i", i=4),
             )
+
+        def quantise(g):
             codes[g] = work.tile([P, GROUP], U32, name="codes", align_bytes=64)
             scales[g] = work.tile([P, GROUP], U8, name="scales", align_bytes=64)
             nc.vector.quantize_mx(
                 out=codes[g][:].bitcast(FP8X4),
                 scales=scales[g][:],
-                in_=grouped[:].rearrange("p w j -> p (w j)"),
+                in_=grouped[g][:].rearrange("p w j -> p (w j)"),
             )
 
-        def start_unit(u):
+        def fill(u, s):
             g, w = divmod(u, 3)
-            for s in range(TILES):
-                acc[u, s] = psum_out.tile([P, C], F32, name="acc")
-                nc.tensor.matmul_mx(
-                    out=acc[u, s][:],
-                    lhsT=codes[g][:, s * P : (s + 1) * P].bitcast(FP8X4),
-                    lhsT_scale=scales[g][:, s * P : (s + 1) * P],
-                    rhs=w_codes[:, w, :].bitcast(FP8X4),
-                    rhs_scale=w_scales[:, w, :],
-                    start=True,
-                    stop=True,
+            acc[u, s] = psum_out.tile([P, C], F32, name="acc")
+            nc.tensor.matmul_mx(
+                out=acc[u, s][:],
+                lhsT=codes[g][:, s * P : (s + 1) * P].bitcast(FP8X4),
+                lhsT_scale=scales[g][:, s * P : (s + 1) * P],
+                rhs=w_codes[:, w, :].bitcast(FP8X4),
+                rhs_scale=w_scales[:, w, :],
+                start=True,
+                stop=True,
+            )
+
+        def drain(u, s):
+            g, w = divmod(u, 3)
+            if s == 0:
+                result[u] = results.tile([P, TILES, C], F32, name="result")
+            nc.vector.tensor_tensor(out=result[u][:, s, :], in0=acc[u, s][:], in1=bias_bc[:, w, :], op=ALU.add)
+            if s == TILES - 1:
+                n, part = divmod(g, PIXELS // GROUP)
+                rows = slice(part * GROUP, (part + 1) * GROUP)
+                nc.sync.dma_start(
+                    out=outs[w][n, rows, :].rearrange("(q s) o -> q s o", s=TILES), in_=result[u][:]
                 )
 
-        def finish_unit(u):
-            g, w = divmod(u, 3)
-            n, part = divmod(g, PIXELS // GROUP)
-            rows = slice(part * GROUP, (part + 1) * GROUP)
-            result = results.tile([P, TILES, C], F32, name="result")
-            nc.vector.tensor_tensor(out=result[:, 0, :], in0=acc[u, 0][:], in1=bias_bc[:, w, :], op=ALU.add)
-            nc.scalar.copy(out=result[:, 1, :], in_=acc[u, 1][:])
-            nc.gpsimd.tensor_tensor(out=result[:, 1, :], in0=result[:, 1, :], in1=bias_bc[:, w, :], op=ALU.add)
-            nc.sync.dma_start(out=outs[w][n, rows, :].rearrange("(q s) o -> q s o", s=TILES), in_=result[:])
-
         def turn_over(u):
-            if 0 <= u - 2 < UNITS:
-                finish_unit(u - 2)
-            if 0 <= u < UNITS:
-                start_unit(u)
+            for s in range(TILES):
+                if 0 <= u - 1 < UNITS:
+                    drain(u - 1, s)
+                if 0 <= u < UNITS:
+                    fill(u, s)
 
         def is_group(g):
             return 0 <= g < GROUPS
@@ -223,23 +254,23 @@ def tile_selfscaleddotproductattention2d_pa_t_kernel(
             if is_group(r):
                 normalise(r)
             if is_group(r - 2):
-                regroup_and_quantise(r - 2)
+                regroup(r - 2, 0, nc.vector.tensor_copy)
+                quantise(r - 2)
             if is_group(r + 2):
                 to_pixel_layout(r + 2)
             turn_over(3 * (r - 2))
 
             if is_group(r + 1):
-                root(r + 1)
-            if is_group(r - 1):
-                gain_and_shift(r - 1, 0)
-            if is_group(r + 1):
-                scale_and_shift(r + 1)
+                deviation(r + 1)
             turn_over(3 * (r - 2) + 1)
 
-            if is_group(r - 1):
-                gain_and_shift(r - 1, 1)
+            if is_group(r + 1):
+                scale_and_shift(r + 1)
             if is_group(r + 2):
-                statistics(r + 2)
+                centre(r + 2)
+            if is_group(r - 1):
+                gain_and_shift(r - 1)
+                regroup(r - 1, 1, nc.scalar.copy)
             if is_group(r):
                 to_channel_layout(r)
             turn_over(3 * (r - 2) + 2)

@@ -50,7 +50,10 @@ def tile_selfscaleddotproductattention2d_pa_t_kernel(
             x_sb.append(keep.tile([P, PACK, PIXELS], BF16, name="x_sb%d" % n))
         for w in range(3):
             w_sb.append(keep.tile([P, C // P, C], BF16, name="w_sb%d" % w))
-        nc.sync.dma_start(out=x_sb[0][:], in_=x[0].rearrange("(p j) h w -> p j (h w)", j=PACK))
+        first_image = x[0].rearrange("(p j) h w -> p j (h w)", j=PACK)
+        for g in range(PIXELS // GROUP):
+            cols = slice(g * GROUP, (g + 1) * GROUP)
+            nc.sync.dma_start(out=x_sb[0][:, :, cols], in_=first_image[:, :, cols])
         for w in range(3):
             nc.sync.dma_start(out=w_sb[w][:], in_=weights[w].rearrange("(a p) c -> p a c", p=P))
         for n in range(1, IMAGES):
@@ -96,7 +99,7 @@ def tile_selfscaleddotproductattention2d_pa_t_kernel(
                         nc.tensor.transpose(
                             bank[:, u, a * P : (a + 1) * P], words[:, 2 * half + a, u, :], ident_f32[:]
                         )
-                nc.scalar.copy(
+                nc.vector.tensor_copy(
                     out=pairs[:, 2 * half * P : 2 * (half + 1) * P, :],
                     in_=bank[:].rearrange("p u o -> p o u"),
                 )
@@ -143,7 +146,7 @@ def tile_selfscaleddotproductattention2d_pa_t_kernel(
 
         def centre(g):
             minus_mean[g] = small.tile([P, TILES], F32, name="minus_mean")
-            nc.vector.tensor_scalar_mul(out=minus_mean[g][:], in0=sums[g][:, :, 0], scalar1=-1.0 / C)
+            nc.scalar.mul(out=minus_mean[g][:], in_=sums[g][:, :, 0], mul=-1.0 / C)
 
         def deviation(g):
             squares[g] = small.tile([P, TILES], F32, name="squares")
@@ -160,11 +163,16 @@ def tile_selfscaleddotproductattention2d_pa_t_kernel(
                 )
             nc.scalar.activation(out=std[g][:], in_=squares[g][:], func=ACT.Sqrt, bias=eps[:], scale=1.0 / C)
 
-        def scale_and_shift(g):
+        def invert(g):
             rstd[g] = small.tile([P, TILES], F32, name="rstd")
-            shift[g] = small.tile([P, TILES], F32, name="shift")
             nc.vector.reciprocal(out=rstd[g][:], in_=std[g][:])
-            nc.vector.tensor_tensor(out=shift[g][:], in0=minus_mean[g][:], in1=rstd[g][:], op=ALU.mult)
+
+        def shift_of(g):
+            shift[g] = small.tile([P, TILES], F32, name="shift")
+            for i in range(TILES):
+                nc.scalar.mul(
+                    out=shift[g][:, i : i + 1], in_=minus_mean[g][:, i : i + 1], mul=rstd[g][:, i : i + 1]
+                )
 
         def normalise(g):
             x_hat[g] = work.tile([P, TILES, PACK, P], F32, name="x_hat")
@@ -197,14 +205,18 @@ def tile_selfscaleddotproductattention2d_pa_t_kernel(
                     bias=beta[:, j : j + 1],
                 )
 
-        def regroup(g, s, copy):
-            if s == TILES - 1:
-                grouped[g] = work.tile([P, GROUP, PACK], BF16, name="grouped", align_bytes=64)
-            cols = slice(s * P, (s + 1) * P)
-            copy(
-                out=grouped[g][:, cols, :].rearrange("p (c i) j -> p c j i", i=4),
-                in_=planes[g][:, :, cols].rearrange("p j (c i) -> p c j i", i=4),
-            )
+        def regroup(g):
+            grouped[g] = work.tile([P, GROUP, PACK], BF16, name="grouped", align_bytes=64)
+            for s in range(TILES):
+                cols = slice(s * P, (s + 1) * P)
+                nc.gpsimd.tensor_scalar(
+                    out=grouped[g][:, cols, :],
+                    in0=planes[g][:, :, cols].rearrange("p j w -> p w j"),
+                    scalar1=1.0,
+                    scalar2=0.0,
+                    op0=ALU.mult,
+                    op1=ALU.add,
+                )
 
         def quantise(g):
             codes[g] = work.tile([P, GROUP], U32, name="codes", align_bytes=64)
@@ -253,27 +265,27 @@ def tile_selfscaleddotproductattention2d_pa_t_kernel(
         for r in range(-2, GROUPS + 3):
             if is_group(r):
                 normalise(r)
-            if is_group(r - 2):
-                regroup(r - 2, 0, nc.vector.tensor_copy)
-                quantise(r - 2)
+            if is_group(r + 1):
+                invert(r + 1)
+            turn_over(3 * (r - 2) - 1)
             if is_group(r + 2):
                 to_pixel_layout(r + 2)
-            turn_over(3 * (r - 2))
 
-            if is_group(r + 1):
-                deviation(r + 1)
-            turn_over(3 * (r - 2) + 1)
-
-            if is_group(r + 1):
-                scale_and_shift(r + 1)
-            if is_group(r + 2):
-                centre(r + 2)
             if is_group(r - 1):
                 gain_and_shift(r - 1)
-                regroup(r - 1, 1, nc.scalar.copy)
+                regroup(r - 1)
+            if is_group(r - 2):
+                quantise(r - 2)
+            turn_over(3 * (r - 2))
             if is_group(r):
                 to_channel_layout(r)
-            turn_over(3 * (r - 2) + 2)
+
+            if is_group(r + 1):
+                shift_of(r + 1)
+            if is_group(r + 2):
+                centre(r + 2)
+                deviation(r + 2)
+            turn_over(3 * (r - 2) + 1)
 
             if 0 <= r + 1 < 3:
                 prepare_weight(r + 1)

@@ -262,30 +262,30 @@ def tile_selfscaleddotproductattention2d_pa_t_kernel(
         def is_group(g):
             return 0 <= g < GROUPS
 
-        for r in range(-2, GROUPS + 3):
+        for r in range(-2, GROUPS + 2):
             if is_group(r):
                 normalise(r)
-            if is_group(r + 1):
-                invert(r + 1)
-            turn_over(3 * (r - 2) - 1)
-            if is_group(r + 2):
-                to_pixel_layout(r + 2)
-
-            if is_group(r - 1):
-                gain_and_shift(r - 1)
-                regroup(r - 1)
-            if is_group(r - 2):
-                quantise(r - 2)
-            turn_over(3 * (r - 2))
+            turn_over(3 * (r - 1) - 1)
             if is_group(r):
                 to_channel_layout(r)
 
             if is_group(r + 1):
-                shift_of(r + 1)
+                centre(r + 1)
+                deviation(r + 1)
+            if is_group(r - 1):
+                quantise(r - 1)
+            turn_over(3 * (r - 1))
             if is_group(r + 2):
-                centre(r + 2)
-                deviation(r + 2)
-            turn_over(3 * (r - 2) + 1)
+                to_pixel_layout(r + 2)
 
-            if 0 <= r + 1 < 3:
-                prepare_weight(r + 1)
+            if is_group(r + 1):
+                invert(r + 1)
+            if is_group(r):
+                gain_and_shift(r)
+                regroup(r)
+            if is_group(r + 1):
+                shift_of(r + 1)
+            turn_over(3 * (r - 1) + 1)
+
+            if 0 <= r + 2 < 3:
+                prepare_weight(r + 2)

@@ -146,7 +146,7 @@ def tile_selfscaleddotproductattention2d_pa_t_kernel(
 
         def centre(g):
             minus_mean[g] = small.tile([P, TILES], F32, name="minus_mean")
-            nc.scalar.mul(out=minus_mean[g][:], in_=sums[g][:, :, 0], mul=-1.0 / C)
+            nc.vector.tensor_scalar_mul(out=minus_mean[g][:], in0=sums[g][:, :, 0], scalar1=-1.0 / C)
 
         def deviation(g):
             squares[g] = small.tile([P, TILES], F32, name="squares")
@@ -163,16 +163,11 @@ def tile_selfscaleddotproductattention2d_pa_t_kernel(
                 )
             nc.scalar.activation(out=std[g][:], in_=squares[g][:], func=ACT.Sqrt, bias=eps[:], scale=1.0 / C)
 
-        def invert(g):
+        def scale_and_shift(g):
             rstd[g] = small.tile([P, TILES], F32, name="rstd")
-            nc.vector.reciprocal(out=rstd[g][:], in_=std[g][:])
-
-        def shift_of(g):
             shift[g] = small.tile([P, TILES], F32, name="shift")
-            for i in range(TILES):
-                nc.scalar.mul(
-                    out=shift[g][:, i : i + 1], in_=minus_mean[g][:, i : i + 1], mul=rstd[g][:, i : i + 1]
-                )
+            nc.vector.reciprocal(out=rstd[g][:], in_=std[g][:])
+            nc.vector.tensor_tensor(out=shift[g][:], in0=minus_mean[g][:], in1=rstd[g][:], op=ALU.mult)
 
         def normalise(g):
             x_hat[g] = work.tile([P, TILES, PACK, P], F32, name="x_hat")
@@ -198,8 +193,8 @@ def tile_selfscaleddotproductattention2d_pa_t_kernel(
             planes[g] = work.tile([P, PACK, GROUP], BF16, name="planes")
             for j in range(PACK):
                 nc.scalar.activation(
-                    out=planes[g][:, j, :].rearrange("p (s q) -> p s q", s=TILES),
-                    in_=plane_bank[g, j // 2][:, j % 2, :].rearrange("p (q s) -> p s q", s=TILES),
+                    out=planes[g][:, j, :],
+                    in_=plane_bank[g, j // 2][:, j % 2, :],
                     func=ACT.Identity,
                     scale=gamma[:, j : j + 1],
                     bias=beta[:, j : j + 1],
@@ -249,7 +244,7 @@ def tile_selfscaleddotproductattention2d_pa_t_kernel(
                 n, part = divmod(g, PIXELS // GROUP)
                 rows = slice(part * GROUP, (part + 1) * GROUP)
                 nc.sync.dma_start(
-                    out=outs[w][n, rows, :].rearrange("(q s) o -> q s o", s=TILES), in_=result[u][:]
+                    out=outs[w][n, rows, :].rearrange("(s q) o -> q s o", s=TILES), in_=result[u][:]
                 )
 
         def turn_over(u):
@@ -265,12 +260,13 @@ def tile_selfscaleddotproductattention2d_pa_t_kernel(
         for r in range(-2, GROUPS + 2):
             if is_group(r):
                 normalise(r)
+            if is_group(r + 1):
+                centre(r + 1)
             turn_over(3 * (r - 1) - 1)
             if is_group(r):
                 to_channel_layout(r)
 
             if is_group(r + 1):
-                centre(r + 1)
                 deviation(r + 1)
             if is_group(r - 1):
                 quantise(r - 1)
@@ -279,12 +275,10 @@ def tile_selfscaleddotproductattention2d_pa_t_kernel(
                 to_pixel_layout(r + 2)
 
             if is_group(r + 1):
-                invert(r + 1)
+                scale_and_shift(r + 1)
             if is_group(r):
                 gain_and_shift(r)
                 regroup(r)
-            if is_group(r + 1):
-                shift_of(r + 1)
             turn_over(3 * (r - 1) + 1)
 
             if 0 <= r + 2 < 3:

@@ -51,11 +51,16 @@ def tile_selfscaleddotproductattention2d_pa_t_kernel(
         for w in range(3):
             w_sb.append(keep.tile([P, C // P, C], BF16, name="w_sb%d" % w))
         first_image = x[0].rearrange("(p j) h w -> p j (h w)", j=PACK)
-        for g in range(PIXELS // GROUP):
+        def load_first_image(g):
             cols = slice(g * GROUP, (g + 1) * GROUP)
             nc.sync.dma_start(out=x_sb[0][:, :, cols], in_=first_image[:, :, cols])
+
+        load_first_image(0)
+        load_first_image(1)
         for w in range(3):
             nc.sync.dma_start(out=w_sb[w][:], in_=weights[w].rearrange("(a p) c -> p a c", p=P))
+        load_first_image(2)
+        load_first_image(3)
         for n in range(1, IMAGES):
             nc.sync.dma_start(out=x_sb[n][:], in_=x[n].rearrange("(p j) h w -> p j (h w)", j=PACK))
 
@@ -88,25 +93,32 @@ def tile_selfscaleddotproductattention2d_pa_t_kernel(
         w_codes = keep.tile([P, 3, C], U32, name="w_codes", align_bytes=64)
         w_scales = keep.tile([P, 3, C], U8, name="w_scales", align_bytes=64)
 
-        def prepare_weight(w):
+        w_bank = {}
+        w_grouped = []
+        for w in range(3):
+            w_grouped.append(keep.tile([P, C, PACK], BF16, name="w_grouped%d" % w, align_bytes=64))
+
+        def turn_weight(w, half):
             words = w_sb[w][:].bitcast(F32).rearrange("p a (q u) -> p a u q", u=2)
-            w_grouped = keep.tile([P, C, PACK], BF16, name="w_grouped%d" % w, align_bytes=64)
-            pairs = w_grouped[:].bitcast(F32)
-            for half in range(2):
-                bank = psum_out.tile([P, 2, 2 * P], F32, name="w_bank", tag="acc")
-                for a in range(2):
-                    for u in range(2):
-                        nc.tensor.transpose(
-                            bank[:, u, a * P : (a + 1) * P], words[:, 2 * half + a, u, :], ident_f32[:]
-                        )
-                nc.vector.tensor_copy(
-                    out=pairs[:, 2 * half * P : 2 * (half + 1) * P, :],
-                    in_=bank[:].rearrange("p u o -> p o u"),
-                )
+            w_bank[w, half] = psum_out.tile([P, 2, 2 * P], F32, name="w_bank", tag="acc")
+            for a in range(2):
+                for u in range(2):
+                    nc.tensor.transpose(
+                        w_bank[w, half][:, u, a * P : (a + 1) * P], words[:, 2 * half + a, u, :], ident_f32[:]
+                    )
+
+        def group_weight(w, half):
+            pairs = w_grouped[w][:].bitcast(F32)
+            nc.vector.tensor_copy(
+                out=pairs[:, 2 * half * P : 2 * (half + 1) * P, :],
+                in_=w_bank[w, half][:].rearrange("p u o -> p o u"),
+            )
+
+        def quantise_weight(w):
             nc.vector.quantize_mx(
                 out=w_codes[:, w, :].bitcast(FP8X4),
                 scales=w_scales[:, w, :],
-                in_=w_grouped[:].rearrange("p o t -> p (o t)"),
+                in_=w_grouped[w][:].rearrange("p o t -> p (o t)"),
             )
 
         x_t = {}
@@ -257,11 +269,41 @@ def tile_selfscaleddotproductattention2d_pa_t_kernel(
         def is_group(g):
             return 0 <= g < GROUPS
 
-        for r in range(-2, GROUPS + 2):
+        for g in range(2):
+            to_pixel_layout(g)
+            centre(g)
+        deviation(0)
+        scale_and_shift(0)
+        turn_weight(0, 0)
+        turn_weight(0, 1)
+        turn_weight(1, 0)
+        group_weight(0, 0)
+        turn_weight(1, 1)
+        group_weight(0, 1)
+        quantise_weight(0)
+
+        normalise(0)
+        to_channel_layout(0)
+        turn_weight(2, 0)
+        deviation(1)
+        group_weight(1, 0)
+        turn_weight(2, 1)
+        to_pixel_layout(2)
+        group_weight(1, 1)
+        scale_and_shift(1)
+        quantise_weight(1)
+        group_weight(2, 0)
+        group_weight(2, 1)
+        gain_and_shift(0)
+        regroup(0)
+
+        for r in range(1, GROUPS + 2):
             if is_group(r):
                 normalise(r)
             if is_group(r + 1):
                 centre(r + 1)
+            if r == 1:
+                quantise_weight(2)
             turn_over(3 * (r - 1) - 1)
             if is_group(r):
                 to_channel_layout(r)
@@ -280,6 +322,3 @@ def tile_selfscaleddotproductattention2d_pa_t_kernel(
                 gain_and_shift(r)
                 regroup(r)
             turn_over(3 * (r - 1) + 1)
-
-            if 0 <= r + 2 < 3:
-                prepare_weight(r + 2)

@@ -297,22 +297,20 @@ def tile_selfscaleddotproductattention2d_pa_t_kernel(
         gain_and_shift(0)
         regroup(0)
 
-        for r in range(1, GROUPS + 2):
+        for r in range(1, GROUPS + 3):
             if is_group(r):
                 normalise(r)
             if is_group(r + 1):
                 centre(r + 1)
             if r == 1:
                 quantise_weight(2)
-            turn_over(3 * (r - 1) - 1)
+            turn_over(3 * (r - 1) - 2)
             if is_group(r):
                 to_channel_layout(r)
 
             if is_group(r + 1):
                 deviation(r + 1)
-            if is_group(r - 1):
-                quantise(r - 1)
-            turn_over(3 * (r - 1))
+            turn_over(3 * (r - 1) - 1)
             if is_group(r + 2):
                 to_pixel_layout(r + 2)
 
@@ -321,4 +319,6 @@ def tile_selfscaleddotproductattention2d_pa_t_kernel(
             if is_group(r):
                 gain_and_shift(r)
                 regroup(r)
-            turn_over(3 * (r - 1) + 1)
+            if is_group(r - 1):
+                quantise(r - 1)
+            turn_over(3 * (r - 1))

@@ -215,10 +215,9 @@ def tile_selfscaleddotproductattention2d_pa_t_kernel(
         def regroup(g):
             grouped[g] = work.tile([P, GROUP, PACK], BF16, name="grouped", align_bytes=64)
             for s in range(TILES):
-                cols = slice(s * P, (s + 1) * P)
                 nc.gpsimd.tensor_scalar(
-                    out=grouped[g][:, cols, :],
-                    in0=planes[g][:, :, cols].rearrange("p j w -> p w j"),
+                    out=grouped[g][:, s * P : (s + 1) * P, :],
+                    in0=planes[g][:].rearrange("p j (w s) -> p s w j", s=TILES)[:, s],
                     scalar1=1.0,
                     scalar2=0.0,
                     op0=ALU.mult,
@@ -256,7 +255,7 @@ def tile_selfscaleddotproductattention2d_pa_t_kernel(
                 n, part = divmod(g, PIXELS // GROUP)
                 rows = slice(part * GROUP, (part + 1) * GROUP)
                 nc.sync.dma_start(
-                    out=outs[w][n, rows, :].rearrange("(s q) o -> q s o", s=TILES), in_=result[u][:]
+                    out=outs[w][n, rows, :].rearrange("(q s) o -> q s o", s=TILES), in_=result[u][:]
                 )
 
         def turn_over(u):

@@ -70,14 +70,20 @@ def tile_selfscaleddotproductattention2d_pa_t_kernel(
         with nc.allow_non_contiguous_dma(reason="four channels of gain and shift to a partition"):
             nc.scalar.dma_start(out=gamma_bf[:], in_=ln_gamma.rearrange("(p j) -> p j", j=PACK))
             nc.scalar.dma_start(out=beta_bf[:], in_=ln_beta.rearrange("(p j) -> p j", j=PACK))
+        bias_in = keep.tile([1, 3, C], BF16, name="bias_in")
+        bias_rows = keep.tile([P, 3, C], BF16, name="bias_rows")
         for w in range(3):
-            nc.scalar.dma_start(out=bias_bc[:, w, :], in_=biases[w].partition_broadcast(P))
+            nc.scalar.dma_start(out=bias_in[:, w, :], in_=biases[w].rearrange("(a o) -> a o", a=1))
+        nc.gpsimd.memset(bias_rows[:], 0.0)
 
         ident_bf = keep.tile([P, P], BF16, name="ident_bf")
         ident_f32 = keep.tile([P, P], F32, name="ident_f32")
         make_identity(nc, ident_bf[:])
         make_identity(nc, ident_f32[:])
-        ones_bf = keep.tile([P, 2], BF16, name="ones_bf")
+        nc.gpsimd.tensor_scalar(
+            out=bias_rows[0:1], in0=bias_in[:], scalar1=1.0, scalar2=0.0, op0=ALU.mult, op1=ALU.add
+        )
+        ones_bf = keep.tile([P, P], BF16, name="ones_bf")
         one = keep.tile([P, 1], F32, name="one")
         eps = keep.tile([P, 1], F32, name="eps")
         warm = keep.tile([P, 1], F32, name="warm")
@@ -92,6 +98,15 @@ def tile_selfscaleddotproductattention2d_pa_t_kernel(
 
         w_codes = keep.tile([P, 3, C], U32, name="w_codes", align_bytes=64)
         w_scales = keep.tile([P, 3, C], U8, name="w_scales", align_bytes=64)
+
+        bias_bank = {}
+
+        def spread_bias(w):
+            bias_bank[w] = psum_out.tile([P, C], F32, name="bias_bank", tag="acc")
+            nc.tensor.matmul(out=bias_bank[w][:], lhsT=ones_bf[:], rhs=bias_rows[:, w, :], start=True, stop=True)
+
+        def keep_bias(w):
+            nc.vector.tensor_copy(out=bias_bc[:, w, :], in_=bias_bank[w][:])
 
         w_bank = {}
         w_grouped = []
@@ -151,7 +166,7 @@ def tile_selfscaleddotproductattention2d_pa_t_kernel(
                     nc.tensor.matmul(
                         out=sums[g][:, i, :],
                         lhsT=x_sb[n][:, j, first : first + P],
-                        rhs=ones_bf[:],
+                        rhs=ones_bf[:, 0:2],
                         start=(j == 0),
                         stop=(j == PACK - 1),
                     )
@@ -293,6 +308,8 @@ def tile_selfscaleddotproductattention2d_pa_t_kernel(
         quantise_weight(1)
         group_weight(2, 0)
         group_weight(2, 1)
+        for w in range(3):
+            spread_bias(w)
         gain_and_shift(0)
         regroup(0)
 
@@ -303,6 +320,8 @@ def tile_selfscaleddotproductattention2d_pa_t_kernel(
                 centre(r + 1)
             if r == 1:
                 quantise_weight(2)
+                for w in range(3):
+                    keep_bias(w)
             turn_over(3 * (r - 1) - 2)
             if is_group(r):
                 to_channel_layout(r)

@@ -101,12 +101,15 @@ def tile_selfscaleddotproductattention2d_pa_t_kernel(
 
         bias_bank = {}
 
-        def spread_bias(w):
-            bias_bank[w] = psum_out.tile([P, C], F32, name="bias_bank", tag="acc")
-            nc.tensor.matmul(out=bias_bank[w][:], lhsT=ones_bf[:], rhs=bias_rows[:, w, :], start=True, stop=True)
+        def spread_bias(first, count):
+            bias_bank[first] = psum_out.tile([P, count, C], BF16, name="bias_bank", tag="acc")
+            for w in range(first, first + count):
+                nc.tensor.matmul(
+                    out=bias_bank[first][:, w - first, :], lhsT=ones_bf[:], rhs=bias_rows[:, w, :], start=True, stop=True
+                )
 
-        def keep_bias(w):
-            nc.vector.tensor_copy(out=bias_bc[:, w, :], in_=bias_bank[w][:])
+        def keep_bias(first, count):
+            nc.vector.tensor_copy(out=bias_bc[:, first : first + count, :], in_=bias_bank[first][:])
 
         w_bank = {}
         w_grouped = []
@@ -155,11 +158,14 @@ def tile_selfscaleddotproductattention2d_pa_t_kernel(
         def to_pixel_layout(g):
             n, part = divmod(g, PIXELS // GROUP)
             x_t[g] = psum_pixel.tile([P, TILES, PACK, P], BF16, name="x_t")
-            sums[g] = psum_sums.tile([P, TILES, 2], F32, name="sums")
             for i in range(TILES):
                 first = part * GROUP + i * P
                 for j in range(PACK):
                     nc.tensor.transpose(x_t[g][:, i, j, :], x_sb[n][:, j, first : first + P], ident_bf[:])
+
+        def add_up(g):
+            n, part = divmod(g, PIXELS // GROUP)
+            sums[g] = psum_sums.tile([P, TILES, 2], F32, name="sums")
             for i in range(TILES):
                 first = part * GROUP + i * P
                 for j in range(PACK):
@@ -273,19 +279,22 @@ def tile_selfscaleddotproductattention2d_pa_t_kernel(
                     out=outs[w][n, rows, :].rearrange("(q s) o -> q s o", s=TILES), in_=result[u][:]
                 )
 
-        def turn_over(u):
+        def turn_over(u, between=None):
             for s in range(TILES):
                 if 0 <= u - 1 < UNITS:
                     drain(u - 1, s)
                 if 0 <= u < UNITS:
                     fill(u, s)
+                if s == 0 and between is not None:
+                    scale_and_shift(between)
 
         def is_group(g):
             return 0 <= g < GROUPS
 
         for g in range(2):
-            to_pixel_layout(g)
+            add_up(g)
             centre(g)
+            to_pixel_layout(g)
         deviation(0)
         scale_and_shift(0)
         turn_weight(0, 0)
@@ -303,13 +312,14 @@ def tile_selfscaleddotproductattention2d_pa_t_kernel(
         group_weight(1, 0)
         turn_weight(2, 1)
         to_pixel_layout(2)
+        add_up(2)
         group_weight(1, 1)
         scale_and_shift(1)
         quantise_weight(1)
         group_weight(2, 0)
         group_weight(2, 1)
-        for w in range(3):
-            spread_bias(w)
+        spread_bias(0, 2)
+        spread_bias(2, 1)
         gain_and_shift(0)
         regroup(0)
 
@@ -320,8 +330,8 @@ def tile_selfscaleddotproductattention2d_pa_t_kernel(
                 centre(r + 1)
             if r == 1:
                 quantise_weight(2)
-                for w in range(3):
-                    keep_bias(w)
+                keep_bias(0, 2)
+                keep_bias(2, 1)
             turn_over(3 * (r - 1) - 2)
             if is_group(r):
                 to_channel_layout(r)
@@ -330,13 +340,13 @@ def tile_selfscaleddotproductattention2d_pa_t_kernel(
                 deviation(r + 1)
             turn_over(3 * (r - 1) - 1)
             if is_group(r + 2):
-                to_pixel_layout(r + 2)
+                add_up(r + 2)
 
-            if is_group(r + 1):
-                scale_and_shift(r + 1)
             if is_group(r):
                 gain_and_shift(r)
                 regroup(r)
             if is_group(r - 1):
                 quantise(r - 1)
-            turn_over(3 * (r - 1))
+            turn_over(3 * (r - 1), r + 1 if is_group(r + 1) else None)
+            if is_group(r + 2):
+                to_pixel_layout(r + 2)

from contextlib import ExitStack

import concourse.mybir as mybir
from concourse.masks import make_identity

F32 = mybir.dt.float32
BF16 = mybir.dt.bfloat16
U32 = mybir.dt.uint32
U8 = mybir.dt.uint8
FP8X4 = mybir.dt.float8_e4m3fn_x4
ACT = mybir.ActivationFunctionType
ALU = mybir.AluOpType

P = 128
PACK = 4
IMAGES = 4
C = 512
PIXELS = 1024
GROUP = 256
TILES = GROUP // P
GROUPS = IMAGES * PIXELS // GROUP
UNITS = 3 * GROUPS
EPS = 1e-5

FLOPS = 2 * IMAGES * PIXELS * C * 3 * C


def tile_selfscaleddotproductattention2d_pa_t_kernel(
    tc, x, ln_gamma, ln_beta, Wq, bq, Wk, bk, Wv, bv, out_0, out_1, out_2
):
    nc = tc.nc
    weights = [Wq, Wk, Wv]
    biases = [bq, bk, bv]
    outs = [out_0, out_1, out_2]

    with ExitStack() as ctx:
        ctx.enter_context(tc.manual_schedule())
        keep = ctx.enter_context(tc.tile_pool(name="keep", bufs=1))
        small = ctx.enter_context(tc.tile_pool(name="small", bufs=3))
        work = ctx.enter_context(tc.tile_pool(name="work", bufs=2))
        results = ctx.enter_context(tc.tile_pool(name="results", bufs=6))
        psum_pixel = ctx.enter_context(tc.psum_pool(name="psum_pixel", bufs=2))
        psum_plane = ctx.enter_context(tc.psum_pool(name="psum_plane", bufs=2))
        psum_sums = ctx.enter_context(tc.psum_pool(name="psum_sums", bufs=1))
        psum_out = ctx.enter_context(tc.psum_pool(name="psum_out", bufs=3))

        x_sb = []
        w_sb = []
        for n in range(IMAGES):
            x_sb.append(keep.tile([P, PACK, PIXELS], BF16, name="x_sb%d" % n))
        for w in range(3):
            w_sb.append(keep.tile([P, C // P, C], BF16, name="w_sb%d" % w))
        first_image = x[0].rearrange("(p j) h w -> p j (h w)", j=PACK)
        def load_first_image(g):
            cols = slice(g * GROUP, (g + 1) * GROUP)
            nc.sync.dma_start(out=x_sb[0][:, :, cols], in_=first_image[:, :, cols])

        load_first_image(0)
        load_first_image(1)
        for w in range(3):
            nc.sync.dma_start(out=w_sb[w][:], in_=weights[w].rearrange("(a p) c -> p a c", p=P))
        load_first_image(2)
        load_first_image(3)
        for n in range(1, IMAGES):
            nc.sync.dma_start(out=x_sb[n][:], in_=x[n].rearrange("(p j) h w -> p j (h w)", j=PACK))

        gamma_bf = keep.tile([P, PACK], BF16, name="gamma_bf")
        beta_bf = keep.tile([P, PACK], BF16, name="beta_bf")
        bias_bc = keep.tile([P, 3, C], BF16, name="bias_bc")
        with nc.allow_non_contiguous_dma(reason="four channels of gain and shift to a partition"):
            nc.scalar.dma_start(out=gamma_bf[:], in_=ln_gamma.rearrange("(p j) -> p j", j=PACK))
            nc.scalar.dma_start(out=beta_bf[:], in_=ln_beta.rearrange("(p j) -> p j", j=PACK))
        bias_in = keep.tile([1, 3, C], BF16, name="bias_in")
        bias_rows = keep.tile([P, 3, C], BF16, name="bias_rows")
        for w in range(3):
            nc.scalar.dma_start(out=bias_in[:, w, :], in_=biases[w].rearrange("(a o) -> a o", a=1))
        nc.gpsimd.memset(bias_rows[:], 0.0)

        ident_bf = keep.tile([P, P], BF16, name="ident_bf")
        ident_f32 = keep.tile([P, P], F32, name="ident_f32")
        make_identity(nc, ident_bf[:])
        make_identity(nc, ident_f32[:])
        nc.gpsimd.tensor_scalar(
            out=bias_rows[0:1], in0=bias_in[:], scalar1=1.0, scalar2=0.0, op0=ALU.mult, op1=ALU.add
        )
        ones_bf = keep.tile([P, P], BF16, name="ones_bf")
        one = keep.tile([P, 1], F32, name="one")
        eps = keep.tile([P, 1], F32, name="eps")
        warm = keep.tile([P, 1], F32, name="warm")
        nc.vector.memset(ones_bf[:], 1.0)
        nc.vector.memset(one[:], 1.0)
        nc.vector.tensor_scalar_mul(out=eps[:], in0=one[:], scalar1=EPS)
        nc.scalar.sqrt(out=warm[:], in_=one[:])
        gamma = keep.tile([P, PACK], F32, name="gamma")
        beta = keep.tile([P, PACK], F32, name="beta")
        nc.vector.tensor_copy(out=gamma[:], in_=gamma_bf[:])
        nc.vector.tensor_copy(out=beta[:], in_=beta_bf[:])

        w_codes = keep.tile([P, 3, C], U32, name="w_codes", align_bytes=64)
        w_scales = keep.tile([P, 3, C], U8, name="w_scales", align_bytes=64)

        bias_bank = {}

        def spread_bias(first, count):
            bias_bank[first] = psum_out.tile([P, count, C], BF16, name="bias_bank", tag="acc")
            for w in range(first, first + count):
                nc.tensor.matmul(
                    out=bias_bank[first][:, w - first, :], lhsT=ones_bf[:], rhs=bias_rows[:, w, :], start=True, stop=True
                )

        def keep_bias(first, count):
            nc.vector.tensor_copy(out=bias_bc[:, first : first + count, :], in_=bias_bank[first][:])

        w_bank = {}
        w_grouped = []
        for w in range(3):
            w_grouped.append(keep.tile([P, C, PACK], BF16, name="w_grouped%d" % w, align_bytes=64))

        def turn_weight(w, half):
            words = w_sb[w][:].bitcast(F32).rearrange("p a (q u) -> p a u q", u=2)
            w_bank[w, half] = psum_out.tile([P, 2, 2 * P], F32, name="w_bank", tag="acc")
            for a in range(2):
                for u in range(2):
                    nc.tensor.transpose(
                        w_bank[w, half][:, u, a * P : (a + 1) * P], words[:, 2 * half + a, u, :], ident_f32[:]
                    )

        def group_weight(w, half):
            pairs = w_grouped[w][:].bitcast(F32)
            nc.vector.tensor_copy(
                out=pairs[:, 2 * half * P : 2 * (half + 1) * P, :],
                in_=w_bank[w, half][:].rearrange("p u o -> p o u"),
            )

        def quantise_weight(w):
            nc.vector.quantize_mx(
                out=w_codes[:, w, :].bitcast(FP8X4),
                scales=w_scales[:, w, :],
                in_=w_grouped[w][:].rearrange("p o t -> p (o t)"),
            )

        x_t = {}
        sums = {}
        minus_mean = {}
        squares = {}
        std = {}
        rstd = {}
        shift = {}
        x_hat = {}
        plane_bank = {}
        planes = {}
        grouped = {}
        codes = {}
        scales = {}
        acc = {}
        result = {}

        def to_pixel_layout(g):
            n, part = divmod(g, PIXELS // GROUP)
            x_t[g] = psum_pixel.tile([P, TILES, PACK, P], BF16, name="x_t")
            for i in range(TILES):
                first = part * GROUP + i * P
                for j in range(PACK):
                    nc.tensor.transpose(x_t[g][:, i, j, :], x_sb[n][:, j, first : first + P], ident_bf[:])

        def add_up(g):
            n, part = divmod(g, PIXELS // GROUP)
            sums[g] = psum_sums.tile([P, TILES, 2], F32, name="sums")
            for i in range(TILES):
                first = part * GROUP + i * P
                for j in range(PACK):
                    nc.tensor.matmul(
                        out=sums[g][:, i, :],
                        lhsT=x_sb[n][:, j, first : first + P],
                        rhs=ones_bf[:, 0:2],
                        start=(j == 0),
                        stop=(j == PACK - 1),
                    )

        def centre(g):
            minus_mean[g] = small.tile([P, TILES], F32, name="minus_mean")
            nc.vector.tensor_scalar_mul(out=minus_mean[g][:], in0=sums[g][:, :, 0], scalar1=-1.0 / C)

        def deviation(g):
            squares[g] = small.tile([P, TILES], F32, name="squares")
            std[g] = small.tile([P, TILES], F32, name="std")
            for i in range(TILES):
                unused = work.tile([P, PACK, P], BF16, name="unused")
                nc.scalar.activation(
                    out=unused[:],
                    in_=x_t[g][:, i],
                    func=ACT.Square,
                    bias=minus_mean[g][:, i : i + 1],
                    scale=1.0,
                    accum_out=squares[g][:, i : i + 1],
                )
            nc.scalar.activation(out=std[g][:], in_=squares[g][:], func=ACT.Sqrt, bias=eps[:], scale=1.0 / C)

        def scale_and_shift(g):
            rstd[g] = small.tile([P, TILES], F32, name="rstd")
            shift[g] = small.tile([P, TILES], F32, name="shift")
            nc.vector.reciprocal(out=rstd[g][:], in_=std[g][:])
            nc.vector.tensor_tensor(out=shift[g][:], in0=minus_mean[g][:], in1=rstd[g][:], op=ALU.mult)

        def normalise(g):
            x_hat[g] = work.tile([P, TILES, PACK, P], F32, name="x_hat")
            for i in range(TILES):
                nc.scalar.activation(
                    out=x_hat[g][:, i],
                    in_=x_t[g][:, i],
                    func=ACT.Identity,
                    scale=rstd[g][:, i : i + 1],
                    bias=shift[g][:, i : i + 1],
                )

        def to_channel_layout(g):
            for b in range(2):
                plane_bank[g, b] = psum_plane.tile([P, 2, GROUP], F32, name="plane")
                for j in (2 * b, 2 * b + 1):
                    for i in range(TILES):
                        nc.tensor.transpose(
                            plane_bank[g, b][:, j % 2, i * P : (i + 1) * P], x_hat[g][:, i, j, :], ident_f32[:]
                        )

        def gain_and_shift(g):
            planes[g] = work.tile([P, PACK, GROUP], BF16, name="planes")
            for j in range(PACK):
                nc.scalar.activation(
                    out=planes[g][:, j, :],
                    in_=plane_bank[g, j // 2][:, j % 2, :],
                    func=ACT.Identity,
                    scale=gamma[:, j : j + 1],
                    bias=beta[:, j : j + 1],
                )

        def regroup(g):
            grouped[g] = work.tile([P, GROUP, PACK], BF16, name="grouped", align_bytes=64)
            for s in range(TILES):
                nc.gpsimd.tensor_scalar(
                    out=grouped[g][:, s * P : (s + 1) * P, :],
                    in0=planes[g][:].rearrange("p j (w s) -> p s w j", s=TILES)[:, s],
                    scalar1=1.0,
                    scalar2=0.0,
                    op0=ALU.mult,
                    op1=ALU.add,
                )

        def quantise(g):
            codes[g] = work.tile([P, GROUP], U32, name="codes", align_bytes=64)
            scales[g] = work.tile([P, GROUP], U8, name="scales", align_bytes=64)
            nc.vector.quantize_mx(
                out=codes[g][:].bitcast(FP8X4),
                scales=scales[g][:],
                in_=grouped[g][:].rearrange("p w j -> p (w j)"),
            )

        def fill(u, s):
            g, w = divmod(u, 3)
            acc[u, s] = psum_out.tile([P, C], F32, name="acc")
            nc.tensor.matmul_mx(
                out=acc[u, s][:],
                lhsT=codes[g][:, s * P : (s + 1) * P].bitcast(FP8X4),
                lhsT_scale=scales[g][:, s * P : (s + 1) * P],
                rhs=w_codes[:, w, :].bitcast(FP8X4),
                rhs_scale=w_scales[:, w, :],
                start=True,
                stop=True,
            )

        def drain(u, s):
            g, w = divmod(u, 3)
            if s == 0:
                result[u] = results.tile([P, TILES, C], F32, name="result")
            nc.vector.tensor_tensor(out=result[u][:, s, :], in0=acc[u, s][:], in1=bias_bc[:, w, :], op=ALU.add)
            if s == TILES - 1:
                n, part = divmod(g, PIXELS // GROUP)
                rows = slice(part * GROUP, (part + 1) * GROUP)
                nc.sync.dma_start(
                    out=outs[w][n, rows, :].rearrange("(q s) o -> q s o", s=TILES), in_=result[u][:]
                )

        def turn_over(u, between=None):
            for s in range(TILES):
                if 0 <= u - 1 < UNITS:
                    drain(u - 1, s)
                if 0 <= u < UNITS:
                    fill(u, s)
                if s == 0 and between is not None:
                    scale_and_shift(between)

        def is_group(g):
            return 0 <= g < GROUPS

        for g in range(2):
            add_up(g)
            centre(g)
            to_pixel_layout(g)
        deviation(0)
        scale_and_shift(0)
        turn_weight(0, 0)
        turn_weight(0, 1)
        turn_weight(1, 0)
        group_weight(0, 0)
        turn_weight(1, 1)
        group_weight(0, 1)
        quantise_weight(0)

        normalise(0)
        to_channel_layout(0)
        turn_weight(2, 0)
        deviation(1)
        group_weight(1, 0)
        turn_weight(2, 1)
        to_pixel_layout(2)
        add_up(2)
        group_weight(1, 1)
        scale_and_shift(1)
        quantise_weight(1)
        group_weight(2, 0)
        group_weight(2, 1)
        spread_bias(0, 2)
        spread_bias(2, 1)
        gain_and_shift(0)
        regroup(0)

        for r in range(1, GROUPS + 3):
            if is_group(r):
                normalise(r)
            if is_group(r + 1):
                centre(r + 1)
            if r == 1:
                quantise_weight(2)
                keep_bias(0, 2)
                keep_bias(2, 1)
            turn_over(3 * (r - 1) - 2)
            if is_group(r):
                to_channel_layout(r)

            if is_group(r + 1):
                deviation(r + 1)
            turn_over(3 * (r - 1) - 1)
            if is_group(r + 2):
                add_up(r + 2)

            if is_group(r):
                gain_and_shift(r)
                regroup(r)
            if is_group(r - 1):
                quantise(r - 1)
            turn_over(3 * (r - 1), r + 1 if is_group(r + 1) else None)
            if is_group(r + 2):
                to_pixel_layout(r + 2)
